import numpy as np
import ml_dtypes


def mxq(x, axis, fmt="e4m3"):
    dtype, down = {"e4m3": (ml_dtypes.float8_e4m3fn, 7), "e5m2": (ml_dtypes.float8_e5m2, 14)}[fmt]
    v = np.moveaxis(np.asarray(x, np.float32).astype(ml_dtypes.bfloat16).astype(np.float64), axis, -1)
    blocks = v.reshape(v.shape[:-1] + (-1, 32))
    amax = np.abs(blocks).max(-1, keepdims=True)
    byte = np.maximum(np.where(amax > 0, np.frexp(amax)[1] - 1 + 127, 0) - down, 1)
    scale = np.exp2(byte - 127.0)
    codes = (blocks / scale).astype(np.float32).astype(dtype).astype(np.float64)
    return np.moveaxis((codes * scale).reshape(v.shape), -1, axis)


WIDE = False


def mx_kscale(k):
    if not WIDE:
        return np.ones(k)
    levels = np.array([30, -30])
    if k % 512:
        return np.exp2(np.random.permutation(np.resize(levels, k // 32))).repeat(32)
    a = np.empty((k // 512, 16))
    for p in range(k // 512):
        a[p, :8] = np.random.permutation(np.resize(levels, 8))
        for g in range(8):
            far = levels[np.abs(levels - a[p, g]) >= 10]
            a[p, g + 8] = far[np.random.randint(len(far))]
    return np.exp2(a.ravel()).repeat(32)


BF16 = ml_dtypes.bfloat16


def bf(x):
    return np.asarray(x, np.float32).astype(BF16)


def f64(x):
    return np.asarray(x).astype(np.float64)


B, T, D, H, KV, DH = 2, 256, 2048, 16, 4, 128
THETA = 1000000.0
EPS = 1e-6
HALF = DH // 2


def rms_norm(u, w):
    return w * u / np.sqrt(np.mean(u * u, axis=-1, keepdims=True) + EPS)


def rope(u):
    timescale = THETA ** (2.0 * np.arange(HALF) / DH)
    ang = (np.arange(T)[:, None] / timescale[None, :])[None, :, None, :]
    sin, cos = np.sin(ang), np.cos(ang)
    a, b = u[..., :HALF], u[..., HALF:]
    return np.concatenate([a * cos - b * sin, b * cos + a * sin], axis=-1)


def setup_inputs():
    s = mx_kscale(D)
    small = 3.0 * np.sqrt(EPS / D)
    return {"x": bf(np.random.standard_normal((B, T, D)) * s),
            "wq": bf(np.random.standard_normal((D, H * DH)) * small / s[:, None]),
            "wk": bf(np.random.standard_normal((D, KV * DH)) * small / s[:, None]),
            "wv": bf(np.random.standard_normal((D, KV * DH)) / np.sqrt(D) / s[:, None]),
            "q_norm_w": bf(1.0 + 0.1 * np.random.standard_normal(DH)),
            "k_norm_w": bf(1.0 + 0.1 * np.random.standard_normal(DH))}


def reference(x, wq, wk, wv, q_norm_w, k_norm_w):
    xq = mxq(f64(x), 2, "e5m2")
    q = (xq @ mxq(f64(wq), 0, "e5m2")).reshape(B, T, H, DH)
    k = (xq @ mxq(f64(wk), 0, "e5m2")).reshape(B, T, KV, DH)
    v = (xq @ mxq(f64(wv), 0, "e5m2")).reshape(B, T, KV, DH)
    return rope(rms_norm(q, f64(q_norm_w))), rope(rms_norm(k, f64(k_norm_w))), v

@@ -1,0 +1,243 @@
+import math
+from contextlib import ExitStack
+
+import concourse.mybir as mybir
+from concourse.masks import make_identity
+
+B, T, D, H, KV, DH = 2, 256, 2048, 16, 4, 128
+THETA = 1000000.0
+EPS = 1e-6
+HALF = DH // 2
+FLOPS = 2 * B * T * D * (H + 2 * KV) * DH
+
+F32 = mybir.dt.float32
+BF16 = mybir.dt.bfloat16
+I32 = mybir.dt.int32
+U32 = mybir.dt.uint32
+U8 = mybir.dt.uint8
+E5M2X4 = mybir.dt.float8_e5m2_x4
+ALU = mybir.AluOpType
+ACT = mybir.ActivationFunctionType
+
+P = 128
+PACK = 4
+K_PASS = P * PACK
+PASSES = D // K_PASS
+N = 512
+HEADS = N // DH
+TILES = B * T // P
+CHUNKS = (H + 2 * KV) * DH // N
+BLOCKS = CHUNKS * PASSES
+ROPED = (CHUNKS - 1) * TILES
+RUN = 4
+V_HEAD = 336
+V_STEADY = 192
+
+
+def tile_qwen3attention_pa_kernel(tc, x, wq, wk, wv, q_norm_w, k_norm_w, out_0, out_1, out_2):
+    nc = tc.nc
+    x_rows = x.rearrange("b t d -> (b t) d")
+    q_rows = out_0.rearrange("b t h d -> (b t) (h d)")
+    k_rows = out_1.rearrange("b t h d -> (b t) (h d)")
+    v_rows = out_2.rearrange("b t h d -> (b t) (h d)")
+    q_chunks = H * DH // N
+    chunk_w = [wk] + [wq[:, c * N:(c + 1) * N] for c in range(q_chunks)] + [wv]
+    chunk_out = [k_rows] + [q_rows[:, c * N:(c + 1) * N] for c in range(q_chunks)] + [v_rows]
+
+    with ExitStack() as ctx:
+        keep = ctx.enter_context(tc.tile_pool(name="keep", bufs=1))
+        work = ctx.enter_context(tc.tile_pool(name="work", bufs=2))
+        psum = ctx.enter_context(tc.psum_pool(name="psum", bufs=1))
+        ctx.enter_context(tc.manual_schedule())
+
+        w_raw, x_raw = {}, {}
+        grouped, w_codes, w_scales = {}, {}, {}
+        x_grouped, x_codes, x_scales = {}, {}, {}
+        acc, sum_sq, rstd, prod, result = {}, {}, {}, {}, {}
+
+        def load_w(b):
+            c, g = divmod(b, PASSES)
+            w_raw[b] = keep.tile([P, PACK, N], BF16, name="w_raw%d" % b, align_bytes=64)
+            rows = chunk_w[c][g * K_PASS:(g + 1) * K_PASS, :]
+            nc.sync.dma_start(out=w_raw[b][:], in_=rows.rearrange("(p j) n -> p j n", j=PACK))
+
+        def load_w_pair(b0, b1):
+            c, g = divmod(b0, PASSES)
+            pair = keep.tile([P, PACK, 2 * N], BF16, name="w_pair%d" % b0, align_bytes=64)
+            rows = wq[g * K_PASS:(g + 1) * K_PASS, (c - 1) * N:(c + 1) * N]
+            nc.sync.dma_start(out=pair[:], in_=rows.rearrange("(p j) n -> p j n", j=PACK))
+            w_raw[b0] = pair[:, :, :N]
+            w_raw[b1] = pair[:, :, N:]
+
+        def load_x(m):
+            x_raw[m] = keep.tile([P, D], BF16, name="x_raw%d" % m, align_bytes=64)
+            nc.sync.dma_start(out=x_raw[m][:], in_=x_rows[m * P:(m + 1) * P, :])
+
+        norm_w = keep.tile([P, 2, DH], BF16, name="norm_w")
+        nc.scalar.dma_start(out=norm_w[:, 0, :], in_=k_norm_w.partition_broadcast(P))
+        nc.scalar.dma_start(out=norm_w[:, 1, :], in_=q_norm_w.partition_broadcast(P))
+
+        for i in range(TILES):
+            load_w(i)
+            load_x(i)
+        for c in range(1, q_chunks + 1, 2):
+            for g in range(PASSES):
+                load_w_pair(c * PASSES + g, (c + 1) * PASSES + g)
+        for g in range(PASSES):
+            load_w((CHUNKS - 1) * PASSES + g)
+
+        pos = keep.tile([P, 2], I32, name="pos")
+        nc.gpsimd.iota(pos[:], pattern=[[P, 2]], base=0, channel_multiplier=1)
+        ident = keep.tile([P, P], F32, name="ident")
+        make_identity(nc, ident[:])
+
+        ratio = THETA ** (-2.0 / DH)
+        low = keep.tile([P, 2, 8], F32, name="low")
+        for j in range(8):
+            nc.vector.tensor_scalar(out=low[:, :, j], in0=pos[:], scalar1=ratio ** j / (2 * math.pi), scalar2=None,
+                                    op0=ALU.mult)
+        turns = keep.tile([P, 2, 2, HALF], F32, name="turns")
+        for a in range(8):
+            nc.vector.tensor_scalar(out=turns[:, :, 1, 8 * a:8 * a + 8], in0=low[:], scalar1=ratio ** (8 * a),
+                                    scalar2=None, op0=ALU.mult)
+        nc.vector.tensor_scalar(out=turns[:, :, 0, :], in0=turns[:, :, 1, :], scalar1=0.25, scalar2=None, op0=ALU.add)
+        whole = keep.tile([P, 2, 2, HALF], I32, name="whole")
+        nc.vector.tensor_copy(out=whole[:], in_=turns[:])
+        frac = keep.tile([P, 2, 2, HALF], F32, name="frac")
+        nc.vector.tensor_tensor(out=frac[:], in0=turns[:], in1=whole[:], op=ALU.subtract)
+        trig = keep.tile([P, 4, HALF], F32, name="trig")
+        nc.scalar.activation(out=trig[:], in_=frac[:].rearrange("p a b j -> p (a b) j"), func=ACT.Sin,
+                             scale=2 * math.pi)
+        table = keep.tile([P, 2, 4, DH], F32, name="table")
+
+        def make_table(w):
+            nc.vector.tensor_tensor(
+                out=table[:, w].rearrange("p a (two j) -> p a two j", two=2),
+                in0=trig[:].unsqueeze(2).to_broadcast([P, 4, 2, HALF]),
+                in1=norm_w[:, w, :].rearrange("p (two j) -> p two j", two=2).unsqueeze(1).to_broadcast([P, 4, 2, HALF]),
+                op=ALU.mult)
+
+        def v_share(b):
+            return V_HEAD if b <= PASSES else V_STEADY
+
+        def interleave(engine_copy, b, c0, c1):
+            if b not in grouped:
+                grouped[b] = work.tile([P, N, PACK], BF16, name="grouped", bufs=4, align_bytes=64)
+            engine_copy(out=grouped[b][:, c0:c1, :].rearrange("p (c i) t -> p c t i", i=RUN),
+                        in_=w_raw[b][:, :, c0:c1].rearrange("p t (c i) -> p c t i", i=RUN))
+
+        def interleave_v(b):
+            interleave(nc.vector.tensor_copy, b, 0, v_share(b))
+
+        def interleave_s(b):
+            interleave(nc.scalar.copy, b, v_share(b), N)
+
+        def quantize_w(b):
+            w_codes[b] = work.tile([P, N], U32, name="w_codes", bufs=6, align_bytes=64)
+            w_scales[b] = work.tile([P, N], U8, name="w_scales", bufs=6, align_bytes=64)
+            nc.vector.quantize_mx(out=w_codes[b][:].bitcast(E5M2X4), scales=w_scales[b][:],
+                                  in_=grouped[b][:].rearrange("p n t -> p (n t)"))
+
+        def transpose_x(m):
+            words = x_raw[m][:].bitcast(F32)
+            x_grouped[m] = work.tile([P, PASSES, P, PACK], BF16, name="x_grouped", bufs=2, align_bytes=64)
+            for gp in range(PASSES // 2):
+                bank = psum.tile([P, 2, 2, P], F32, name="xt", tag="bank%d" % (TILES + 2 * (m % 2) + gp))
+                for gl in range(2):
+                    g = 2 * gp + gl
+                    for u in range(2):
+                        nc.tensor.transpose(bank[:, gl, u, :], words[:, 256 * g + u:256 * (g + 1):2], ident[:])
+                dst = x_grouped[m][:, 2 * gp:2 * gp + 2].rearrange("p g r t -> p (g r t)").bitcast(F32)
+                nc.scalar.copy(out=dst.rearrange("p (g r u) -> p g r u", g=2, u=2),
+                               in_=bank[:].rearrange("p g u r -> p g r u"))
+
+        def quantize_x(m):
+            x_codes[m] = keep.tile([P, PASSES, P], U32, name="x_codes%d" % m, align_bytes=64)
+            x_scales[m] = keep.tile([P, PASSES, P], U8, name="x_scales%d" % m, align_bytes=64)
+            nc.vector.quantize_mx(out=x_codes[m][:].rearrange("p g r -> p (g r)").bitcast(E5M2X4),
+                                  scales=x_scales[m][:].rearrange("p g r -> p (g r)"),
+                                  in_=x_grouped[m][:].rearrange("p g r t -> p (g r t)"))
+
+        def matmul(b, m):
+            c, g = divmod(b, PASSES)
+            i = c * TILES + m
+            if g == 0:
+                acc[i] = psum.tile([P, N], F32, name="acc", tag="bank%d" % (i % (2 * TILES)))
+            nc.tensor.matmul_mx(out=acc[i][:], lhsT=x_codes[m][:, g, :].bitcast(E5M2X4), lhsT_scale=x_scales[m][:, g, :],
+                                rhs=w_codes[b][:].bitcast(E5M2X4), rhs_scale=w_scales[b][:],
+                                start=(g == 0), stop=(g == PASSES - 1))
+
+        def square_sums(i):
+            sum_sq[i] = work.tile([P, HEADS], F32, name="sum_sq", bufs=3)
+            squares = work.tile([P, HEADS, DH], F32, name="squares", bufs=2)
+            for h in range(HEADS):
+                nc.scalar.activation(out=squares[:, h, :], in_=acc[i][:, h * DH:(h + 1) * DH], func=ACT.Square,
+                                     accum_out=sum_sq[i][:, h:h + 1])
+
+        def inverse_rms(i):
+            rstd[i] = work.tile([P, HEADS], F32, name="rstd", bufs=3)
+            nc.scalar.activation(out=rstd[i][:], in_=sum_sq[i][:], func=ACT.Abs_reciprocal_sqrt,
+                                 scale=1.0 / DH, bias=EPS)
+
+        def rope_products(i):
+            c, m = divmod(i, TILES)
+            w = min(c, 1)
+            half = m % 2
+            prod[i] = work.tile([P, HEADS, 2, DH], F32, name="prod", bufs=3)
+            for h in range(HEADS):
+                nc.vector.scalar_tensor_tensor(
+                    out=prod[i][:, h], in0=acc[i][:, h * DH:(h + 1) * DH].unsqueeze(1).to_broadcast([P, 2, DH]),
+                    scalar=rstd[i][:, h:h + 1], in1=table[:, w, 2 * half:2 * half + 2, :],
+                    op0=ALU.mult, op1=ALU.mult)
+
+        def store(i):
+            c, m = divmod(i, TILES)
+            nc.sync.dma_start(out=chunk_out[c][m * P:(m + 1) * P, :], in_=result[i][:].rearrange("p h d -> p (h d)"))
+
+        def rope_sums(engine, i):
+            result[i] = work.tile([P, HEADS, DH], F32, name="result", bufs=16)
+            engine.tensor_tensor(out=result[i][:, :, :HALF], in0=prod[i][:, :, 0, :HALF], in1=prod[i][:, :, 1, HALF:],
+                                 op=ALU.subtract)
+            engine.tensor_tensor(out=result[i][:, :, HALF:], in0=prod[i][:, :, 0, HALF:], in1=prod[i][:, :, 1, :HALF],
+                                 op=ALU.add)
+            store(i)
+
+        def copy_out_v(i):
+            result[i] = work.tile([P, HEADS, DH], F32, name="result", bufs=16)
+            nc.scalar.copy(out=result[i][:].rearrange("p h d -> p (h d)"), in_=acc[i][:])
+            store(i)
+
+        make_table(0)
+        for i in range(TILES):
+            interleave_s(i)
+            interleave_v(i)
+            transpose_x(i)
+            quantize_w(i)
+            quantize_x(i)
+            for g in range(i):
+                matmul(g, i)
+            for m in range(i + 1):
+                matmul(i, m)
+        make_table(1)
+        interleave_s(PASSES)
+        interleave_v(PASSES)
+        interleave_s(PASSES + 1)
+
+        for s in range(PASSES, BLOCKS):
+            square_sums(s - PASSES)
+            if s + 2 < BLOCKS:
+                interleave_s(s + 2)
+            inverse_rms(s - PASSES)
+            if s + 1 < BLOCKS:
+                interleave_v(s + 1)
+            quantize_w(s)
+            for m in range(TILES):
+                matmul(s, m)
+            if s > PASSES:
+                rope_products(s - PASSES - 1)
+                rope_sums(nc.gpsimd, s - PASSES - 1)
+
+        rope_products(ROPED - 1)
+        for m in range(TILES):
+            copy_out_v(ROPED + m)
+        rope_sums(nc.vector, ROPED - 1)

@@ -30,7 +30,8 @@ CHUNKS = (H + 2 * KV) * DH // N
 BLOCKS = CHUNKS * PASSES
 ROPED = (CHUNKS - 1) * TILES
 RUN = 4
-V_HEAD = 336
+V_HEAD = 256
+V_FILL = 416
 V_STEADY = 192
 
 
@@ -57,34 +58,29 @@ def tile_qwen3attention_pa_kernel(tc, x, wq, wk, wv, q_norm_w, k_norm_w, out_0, 
 
         def load_w(b):
             c, g = divmod(b, PASSES)
-            w_raw[b] = keep.tile([P, PACK, N], BF16, name="w_raw%d" % b, align_bytes=64)
+            w_raw[b] = keep.tile([P, PACK, N], BF16, name="w_raw", tag="slot%d" % b, align_bytes=64)
             rows = chunk_w[c][g * K_PASS:(g + 1) * K_PASS, :]
             nc.sync.dma_start(out=w_raw[b][:], in_=rows.rearrange("(p j) n -> p j n", j=PACK))
-
-        def load_w_pair(b0, b1):
-            c, g = divmod(b0, PASSES)
-            pair = keep.tile([P, PACK, 2 * N], BF16, name="w_pair%d" % b0, align_bytes=64)
-            rows = wq[g * K_PASS:(g + 1) * K_PASS, (c - 1) * N:(c + 1) * N]
-            nc.sync.dma_start(out=pair[:], in_=rows.rearrange("(p j) n -> p j n", j=PACK))
-            w_raw[b0] = pair[:, :, :N]
-            w_raw[b1] = pair[:, :, N:]
 
         def load_x(m):
             x_raw[m] = keep.tile([P, D], BF16, name="x_raw%d" % m, align_bytes=64)
             nc.sync.dma_start(out=x_raw[m][:], in_=x_rows[m * P:(m + 1) * P, :])
 
-        norm_w = keep.tile([P, 2, DH], BF16, name="norm_w")
-        nc.scalar.dma_start(out=norm_w[:, 0, :], in_=k_norm_w.partition_broadcast(P))
-        nc.scalar.dma_start(out=norm_w[:, 1, :], in_=q_norm_w.partition_broadcast(P))
+        head_order = [("w", 0), ("x", 0), ("x", 1), ("w", 1), ("x", 2), ("x", 3), ("w", 2), ("w", 3)]
+        for kind, i in head_order:
+            (load_w if kind == "w" else load_x)(i)
+        for b in range(PASSES, BLOCKS):
+            load_w(b)
 
-        for i in range(TILES):
-            load_w(i)
-            load_x(i)
-        for c in range(1, q_chunks + 1, 2):
-            for g in range(PASSES):
-                load_w_pair(c * PASSES + g, (c + 1) * PASSES + g)
-        for g in range(PASSES):
-            load_w((CHUNKS - 1) * PASSES + g)
+        norm_rows = keep.tile([P, 2, DH], BF16, name="norm_rows")
+        nc.vector.memset(norm_rows[:], 0.0)
+        ones = keep.tile([P, P], BF16, name="ones")
+        nc.vector.memset(ones[:], 1.0)
+        nc.scalar.dma_start(out=norm_rows[0:1, 0, :], in_=k_norm_w.rearrange("(o d) -> o d", o=1))
+        nc.scalar.dma_start(out=norm_rows[0:1, 1, :], in_=q_norm_w.rearrange("(o d) -> o d", o=1))
+        norm_w = psum.tile([P, 2, DH], F32, name="norm_w", tag="bank0")
+        nc.tensor.matmul(out=norm_w[:].rearrange("p w d -> p (w d)"), lhsT=ones[:],
+                         rhs=norm_rows[:].rearrange("p w d -> p (w d)"), start=True, stop=True)
 
         pos = keep.tile([P, 2], I32, name="pos")
         nc.gpsimd.iota(pos[:], pattern=[[P, 2]], base=0, channel_multiplier=1)
@@ -96,15 +92,17 @@ def tile_qwen3attention_pa_kernel(tc, x, wq, wk, wv, q_norm_w, k_norm_w, out_0, 
         for j in range(8):
             nc.vector.tensor_scalar(out=low[:, :, j], in0=pos[:], scalar1=ratio ** j / (2 * math.pi), scalar2=None,
                                     op0=ALU.mult)
-        turns = keep.tile([P, 2, 2, HALF], F32, name="turns")
+        turns = keep.tile([P, 2, HALF], F32, name="turns")
         for a in range(8):
-            nc.vector.tensor_scalar(out=turns[:, :, 1, 8 * a:8 * a + 8], in0=low[:], scalar1=ratio ** (8 * a),
+            nc.vector.tensor_scalar(out=turns[:, :, 8 * a:8 * a + 8], in0=low[:], scalar1=ratio ** (8 * a),
                                     scalar2=None, op0=ALU.mult)
-        nc.vector.tensor_scalar(out=turns[:, :, 0, :], in0=turns[:, :, 1, :], scalar1=0.25, scalar2=None, op0=ALU.add)
         whole = keep.tile([P, 2, 2, HALF], I32, name="whole")
-        nc.vector.tensor_copy(out=whole[:], in_=turns[:])
         frac = keep.tile([P, 2, 2, HALF], F32, name="frac")
-        nc.vector.tensor_tensor(out=frac[:], in0=turns[:], in1=whole[:], op=ALU.subtract)
+        for cs, shift in enumerate((0.25, 0.0)):
+            nc.vector.tensor_scalar(out=whole[:, :, cs, :], in0=turns[:], scalar1=shift, scalar2=None, op0=ALU.add)
+        for cs, shift in enumerate((0.25, 0.0)):
+            nc.vector.scalar_tensor_tensor(out=frac[:, :, cs, :], in0=turns[:], scalar=shift, in1=whole[:, :, cs, :],
+                                           op0=ALU.add, op1=ALU.subtract)
         trig = keep.tile([P, 4, HALF], F32, name="trig")
         nc.scalar.activation(out=trig[:], in_=frac[:].rearrange("p a b j -> p (a b) j"), func=ACT.Sin,
                              scale=2 * math.pi)
@@ -118,7 +116,9 @@ def tile_qwen3attention_pa_kernel(tc, x, wq, wk, wv, q_norm_w, k_norm_w, out_0, 
                 op=ALU.mult)
 
         def v_share(b):
-            return V_HEAD if b <= PASSES else V_STEADY
+            if b < PASSES:
+                return V_HEAD
+            return V_FILL if b < PASSES + 2 else V_STEADY
 
         def interleave(engine_copy, b, c0, c1):
             if b not in grouped:
@@ -195,7 +195,7 @@ def tile_qwen3attention_pa_kernel(tc, x, wq, wk, wv, q_norm_w, k_norm_w, out_0, 
             nc.sync.dma_start(out=chunk_out[c][m * P:(m + 1) * P, :], in_=result[i][:].rearrange("p h d -> p (h d)"))
 
         def rope_sums(engine, i):
-            result[i] = work.tile([P, HEADS, DH], F32, name="result", bufs=16)
+            result[i] = keep.tile([P, HEADS, DH], F32, name="result", tag="slot%d" % ((i + 7) % BLOCKS), align_bytes=64)
             engine.tensor_tensor(out=result[i][:, :, :HALF], in0=prod[i][:, :, 0, :HALF], in1=prod[i][:, :, 1, HALF:],
                                  op=ALU.subtract)
             engine.tensor_tensor(out=result[i][:, :, HALF:], in0=prod[i][:, :, 0, HALF:], in1=prod[i][:, :, 1, :HALF],
@@ -203,22 +203,26 @@ def tile_qwen3attention_pa_kernel(tc, x, wq, wk, wv, q_norm_w, k_norm_w, out_0, 
             store(i)
 
         def copy_out_v(i):
-            result[i] = work.tile([P, HEADS, DH], F32, name="result", bufs=16)
+            result[i] = keep.tile([P, HEADS, DH], F32, name="result", tag="slot%d" % ((i + 7) % BLOCKS), align_bytes=64)
             nc.scalar.copy(out=result[i][:].rearrange("p h d -> p (h d)"), in_=acc[i][:])
             store(i)
 
         make_table(0)
-        for i in range(TILES):
-            interleave_s(i)
-            interleave_v(i)
-            transpose_x(i)
-            quantize_w(i)
-            quantize_x(i)
-            for g in range(i):
-                matmul(g, i)
-            for m in range(i + 1):
-                matmul(i, m)
         make_table(1)
+        previous = None
+        for kind, i in head_order:
+            if kind == "x":
+                transpose_x(i)
+            else:
+                interleave_s(i)
+                interleave_v(i)
+            if previous is not None:
+                (quantize_w if previous[0] == "w" else quantize_x)(previous[1])
+            previous = (kind, i)
+        quantize_w(PASSES - 1)
+        for g in range(PASSES):
+            for m in range(TILES):
+                matmul(g, m)
         interleave_s(PASSES)
         interleave_v(PASSES)
         interleave_s(PASSES + 1)
@@ -233,10 +237,12 @@ def tile_qwen3attention_pa_kernel(tc, x, wq, wk, wv, q_norm_w, k_norm_w, out_0, 
             quantize_w(s)
             for m in range(TILES):
                 matmul(s, m)
+            if s > PASSES + 1:
+                rope_sums(nc.gpsimd, s - PASSES - 2)
             if s > PASSES:
                 rope_products(s - PASSES - 1)
-                rope_sums(nc.gpsimd, s - PASSES - 1)
 
+        rope_sums(nc.gpsimd, ROPED - 2)
         rope_products(ROPED - 1)
         for m in range(TILES):
             copy_out_v(ROPED + m)

@@ -66,24 +66,20 @@ def tile_qwen3attention_pa_kernel(tc, x, wq, wk, wv, q_norm_w, k_norm_w, out_0, 
             x_raw[m] = keep.tile([P, D], BF16, name="x_raw%d" % m, align_bytes=64)
             nc.sync.dma_start(out=x_raw[m][:], in_=x_rows[m * P:(m + 1) * P, :])
 
-        head_order = [("w", 0), ("x", 0), ("x", 1), ("w", 1), ("x", 2), ("x", 3), ("w", 2), ("w", 3)]
+        head_order = [("x", 0), ("x", 1), ("w", 0), ("x", 2), ("x", 3), ("w", 1), ("w", 2), ("w", 3)]
         for kind, i in head_order:
             (load_w if kind == "w" else load_x)(i)
         for b in range(PASSES, BLOCKS):
             load_w(b)
 
+        pos = keep.tile([P, 2], I32, name="pos")
+        nc.gpsimd.iota(pos[:], pattern=[[P, 2]], base=0, channel_multiplier=1)
         norm_rows = keep.tile([P, 2, DH], BF16, name="norm_rows")
         nc.vector.memset(norm_rows[:], 0.0)
         ones = keep.tile([P, P], BF16, name="ones")
         nc.vector.memset(ones[:], 1.0)
         nc.scalar.dma_start(out=norm_rows[0:1, 0, :], in_=k_norm_w.rearrange("(o d) -> o d", o=1))
         nc.scalar.dma_start(out=norm_rows[0:1, 1, :], in_=q_norm_w.rearrange("(o d) -> o d", o=1))
-        norm_w = psum.tile([P, 2, DH], F32, name="norm_w", tag="bank0")
-        nc.tensor.matmul(out=norm_w[:].rearrange("p w d -> p (w d)"), lhsT=ones[:],
-                         rhs=norm_rows[:].rearrange("p w d -> p (w d)"), start=True, stop=True)
-
-        pos = keep.tile([P, 2], I32, name="pos")
-        nc.gpsimd.iota(pos[:], pattern=[[P, 2]], base=0, channel_multiplier=1)
         ident = keep.tile([P, P], F32, name="ident")
         make_identity(nc, ident[:])
 
@@ -97,23 +93,27 @@ def tile_qwen3attention_pa_kernel(tc, x, wq, wk, wv, q_norm_w, k_norm_w, out_0, 
             nc.vector.tensor_scalar(out=turns[:, :, 8 * a:8 * a + 8], in0=low[:], scalar1=ratio ** (8 * a),
                                     scalar2=None, op0=ALU.mult)
         whole = keep.tile([P, 2, 2, HALF], I32, name="whole")
-        frac = keep.tile([P, 2, 2, HALF], F32, name="frac")
+        frac = keep.tile([P, 2, 3, HALF], F32, name="frac")
         for cs, shift in enumerate((0.25, 0.0)):
             nc.vector.tensor_scalar(out=whole[:, :, cs, :], in0=turns[:], scalar1=shift, scalar2=None, op0=ALU.add)
         for cs, shift in enumerate((0.25, 0.0)):
             nc.vector.scalar_tensor_tensor(out=frac[:, :, cs, :], in0=turns[:], scalar=shift, in1=whole[:, :, cs, :],
                                            op0=ALU.add, op1=ALU.subtract)
-        trig = keep.tile([P, 4, HALF], F32, name="trig")
-        nc.scalar.activation(out=trig[:], in_=frac[:].rearrange("p a b j -> p (a b) j"), func=ACT.Sin,
-                             scale=2 * math.pi)
-        table = keep.tile([P, 2, 4, DH], F32, name="table")
+        nc.vector.tensor_tensor(out=frac[:, :, 2, :], in0=whole[:, :, 1, :], in1=turns[:], op=ALU.subtract)
+        trig = keep.tile([P, 2, 3, HALF], F32, name="trig")
+        nc.scalar.activation(out=trig[:], in_=frac[:], func=ACT.Sin, scale=2 * math.pi)
+        table = keep.tile([P, 2, 2, 2, 2, HALF], F32, name="table")
 
-        def make_table(w):
-            nc.vector.tensor_tensor(
-                out=table[:, w].rearrange("p a (two j) -> p a two j", two=2),
-                in0=trig[:].unsqueeze(2).to_broadcast([P, 4, 2, HALF]),
-                in1=norm_w[:, w, :].rearrange("p (two j) -> p two j", two=2).unsqueeze(1).to_broadcast([P, 4, 2, HALF]),
-                op=ALU.mult)
+        def make_tables():
+            norm_w = psum.tile([P, 2, 2, HALF], F32, name="norm_w", tag="bank0")
+            nc.tensor.matmul(out=norm_w[:].rearrange("p w s j -> p (w s j)"), lhsT=ones[:],
+                             rhs=norm_rows[:].rearrange("p w d -> p (w d)"), start=True, stop=True)
+            for w in range(2):
+                for side in range(2):
+                    nc.vector.tensor_tensor(
+                        out=table[:, w, :, side], in0=trig[:, :, 0:side + 2:side + 1, :],
+                        in1=norm_w[:, w, side, :].unsqueeze(1).unsqueeze(1).to_broadcast([P, 2, 2, HALF]),
+                        op=ALU.mult)
 
         def v_share(b):
             if b < PASSES:
@@ -122,7 +122,7 @@ def tile_qwen3attention_pa_kernel(tc, x, wq, wk, wv, q_norm_w, k_norm_w, out_0, 
 
         def interleave(engine_copy, b, c0, c1):
             if b not in grouped:
-                grouped[b] = work.tile([P, N, PACK], BF16, name="grouped", bufs=4, align_bytes=64)
+                grouped[b] = keep.tile([P, N, PACK], BF16, name="grouped", tag="grouped%d" % (b % 4), align_bytes=64)
             engine_copy(out=grouped[b][:, c0:c1, :].rearrange("p (c i) t -> p c t i", i=RUN),
                         in_=w_raw[b][:, :, c0:c1].rearrange("p t (c i) -> p c t i", i=RUN))
 
@@ -183,34 +183,46 @@ def tile_qwen3attention_pa_kernel(tc, x, wq, wk, wv, q_norm_w, k_norm_w, out_0, 
             c, m = divmod(i, TILES)
             w = min(c, 1)
             half = m % 2
-            prod[i] = work.tile([P, HEADS, 2, DH], F32, name="prod", bufs=3)
+            prod[i] = work.tile([P, 2, N], F32, name="prod", bufs=3)
+            halves = prod[i][:].rearrange("p a (s j) -> p (a s) j", j=HALF)
             for h in range(HEADS):
-                nc.vector.scalar_tensor_tensor(
-                    out=prod[i][:, h], in0=acc[i][:, h * DH:(h + 1) * DH].unsqueeze(1).to_broadcast([P, 2, DH]),
-                    scalar=rstd[i][:, h:h + 1], in1=table[:, w, 2 * half:2 * half + 2, :],
-                    op0=ALU.mult, op1=ALU.mult)
+                for side in range(2):
+                    own = 2 * h + side
+                    partner = 2 * HEADS + 2 * h + 1 - side
+                    nc.vector.scalar_tensor_tensor(
+                        out=halves[:, own:partner + 1:partner - own, :],
+                        in0=acc[i][:, own * HALF:(own + 1) * HALF].unsqueeze(1).to_broadcast([P, 2, HALF]),
+                        scalar=rstd[i][:, h:h + 1], in1=table[:, w, half, side],
+                        op0=ALU.mult, op1=ALU.mult)
+
+        def result_tile(i):
+            last_steady = ROPED - TILES - 2
+            if i == last_steady:
+                tag = "grouped%d" % ((BLOCKS - 2) % 4)
+            elif i < last_steady:
+                tag = "slot%d" % (i + 7)
+            else:
+                tag = "slot%d" % (i - last_steady)
+            result[i] = keep.tile([P, N], F32, name="result", tag=tag, align_bytes=64)
 
         def store(i):
             c, m = divmod(i, TILES)
-            nc.sync.dma_start(out=chunk_out[c][m * P:(m + 1) * P, :], in_=result[i][:].rearrange("p h d -> p (h d)"))
+            nc.sync.dma_start(out=chunk_out[c][m * P:(m + 1) * P, :], in_=result[i][:])
 
         def rope_sums(engine, i):
-            result[i] = keep.tile([P, HEADS, DH], F32, name="result", tag="slot%d" % ((i + 7) % BLOCKS), align_bytes=64)
-            engine.tensor_tensor(out=result[i][:, :, :HALF], in0=prod[i][:, :, 0, :HALF], in1=prod[i][:, :, 1, HALF:],
-                                 op=ALU.subtract)
-            engine.tensor_tensor(out=result[i][:, :, HALF:], in0=prod[i][:, :, 0, HALF:], in1=prod[i][:, :, 1, :HALF],
-                                 op=ALU.add)
+            result_tile(i)
+            engine.tensor_tensor(out=result[i][:], in0=prod[i][:, 0, :], in1=prod[i][:, 1, :], op=ALU.add)
             store(i)
 
         def copy_out_v(i):
-            result[i] = keep.tile([P, HEADS, DH], F32, name="result", tag="slot%d" % ((i + 7) % BLOCKS), align_bytes=64)
-            nc.scalar.copy(out=result[i][:].rearrange("p h d -> p (h d)"), in_=acc[i][:])
+            result_tile(i)
+            nc.scalar.copy(out=result[i][:], in_=acc[i][:])
             store(i)
 
-        make_table(0)
-        make_table(1)
         previous = None
         for kind, i in head_order:
+            if (kind, i) == ("x", 2):
+                make_tables()
             if kind == "x":
                 transpose_x(i)
             else:
@@ -227,13 +239,12 @@ def tile_qwen3attention_pa_kernel(tc, x, wq, wk, wv, q_norm_w, k_norm_w, out_0, 
         interleave_v(PASSES)
         interleave_s(PASSES + 1)
 
-        for s in range(PASSES, BLOCKS):
+        v_first = BLOCKS - PASSES
+        for s in range(PASSES, v_first):
             square_sums(s - PASSES)
-            if s + 2 < BLOCKS:
-                interleave_s(s + 2)
+            interleave_s(s + 2)
             inverse_rms(s - PASSES)
-            if s + 1 < BLOCKS:
-                interleave_v(s + 1)
+            interleave_v(s + 1)
             quantize_w(s)
             for m in range(TILES):
                 matmul(s, m)
@@ -242,8 +253,25 @@ def tile_qwen3attention_pa_kernel(tc, x, wq, wk, wv, q_norm_w, k_norm_w, out_0, 
             if s > PASSES:
                 rope_products(s - PASSES - 1)
 
-        rope_sums(nc.gpsimd, ROPED - 2)
-        rope_products(ROPED - 1)
+        for s in range(v_first, BLOCKS):
+            if s + 2 < BLOCKS:
+                interleave_s(s + 2)
+            if s + 1 < BLOCKS:
+                interleave_v(s + 1)
+            quantize_w(s)
+            for m in range(TILES - 1):
+                matmul(s, m)
+        q_last = ROPED - TILES
+        rope_sums(nc.gpsimd, q_last - 2)
+        rope_products(q_last - 1)
+        for s in range(v_first, BLOCKS):
+            matmul(s, TILES - 1)
         for m in range(TILES):
-            copy_out_v(ROPED + m)
+            square_sums(q_last + m)
+            if m > 0:
+                copy_out_v(ROPED + m - 1)
+            inverse_rms(q_last + m)
+            rope_sums(nc.gpsimd, q_last + m - 1)
+            rope_products(q_last + m)
+        copy_out_v(ROPED + TILES - 1)
         rope_sums(nc.vector, ROPED - 1)

@@ -30,9 +30,11 @@ CHUNKS = (H + 2 * KV) * DH // N
 BLOCKS = CHUNKS * PASSES
 ROPED = (CHUNKS - 1) * TILES
 RUN = 4
-V_HEAD = 256
-V_FILL = 416
-V_STEADY = 192
+V_HEAD = 360
+V_STEADY = 200
+STATS_LAG = 6
+ROPE_LAG = 8
+BANKS = 8
 
 
 def tile_qwen3attention_pa_kernel(tc, x, wq, wk, wv, q_norm_w, k_norm_w, out_0, out_1, out_2):
@@ -66,7 +68,7 @@ def tile_qwen3attention_pa_kernel(tc, x, wq, wk, wv, q_norm_w, k_norm_w, out_0, 
             x_raw[m] = keep.tile([P, D], BF16, name="x_raw%d" % m, align_bytes=64)
             nc.sync.dma_start(out=x_raw[m][:], in_=x_rows[m * P:(m + 1) * P, :])
 
-        head_order = [("x", 0), ("x", 1), ("w", 0), ("x", 2), ("x", 3), ("w", 1), ("w", 2), ("w", 3)]
+        head_order = [(kind, i) for i in range(TILES) for kind in ("w", "x")]
         for kind, i in head_order:
             (load_w if kind == "w" else load_x)(i)
         for b in range(PASSES, BLOCKS):
@@ -116,13 +118,11 @@ def tile_qwen3attention_pa_kernel(tc, x, wq, wk, wv, q_norm_w, k_norm_w, out_0, 
                         op=ALU.mult)
 
         def v_share(b):
-            if b < PASSES:
-                return V_HEAD
-            return V_FILL if b < PASSES + 2 else V_STEADY
+            return V_HEAD if b <= ROPE_LAG + 1 else V_STEADY
 
         def interleave(engine_copy, b, c0, c1):
             if b not in grouped:
-                grouped[b] = keep.tile([P, N, PACK], BF16, name="grouped", tag="grouped%d" % (b % 4), align_bytes=64)
+                grouped[b] = work.tile([P, N, PACK], BF16, name="grouped", bufs=4, align_bytes=64)
             engine_copy(out=grouped[b][:, c0:c1, :].rearrange("p (c i) t -> p c t i", i=RUN),
                         in_=w_raw[b][:, :, c0:c1].rearrange("p t (c i) -> p c t i", i=RUN))
 
@@ -175,7 +175,7 @@ def tile_qwen3attention_pa_kernel(tc, x, wq, wk, wv, q_norm_w, k_norm_w, out_0, 
                                      accum_out=sum_sq[i][:, h:h + 1])
 
         def inverse_rms(i):
-            rstd[i] = work.tile([P, HEADS], F32, name="rstd", bufs=3)
+            rstd[i] = work.tile([P, HEADS], F32, name="rstd", bufs=4)
             nc.scalar.activation(out=rstd[i][:], in_=sum_sq[i][:], func=ACT.Abs_reciprocal_sqrt,
                                  scale=1.0 / DH, bias=EPS)
 
@@ -196,13 +196,7 @@ def tile_qwen3attention_pa_kernel(tc, x, wq, wk, wv, q_norm_w, k_norm_w, out_0, 
                         op0=ALU.mult, op1=ALU.mult)
 
         def result_tile(i):
-            last_steady = ROPED - TILES - 2
-            if i == last_steady:
-                tag = "grouped%d" % ((BLOCKS - 2) % 4)
-            elif i < last_steady:
-                tag = "slot%d" % (i + 7)
-            else:
-                tag = "slot%d" % (i - last_steady)
+            tag = "slot%d" % ((i + ROPE_LAG + 2) % BLOCKS)
             result[i] = keep.tile([P, N], F32, name="result", tag=tag, align_bytes=64)
 
         def store(i):
@@ -221,7 +215,7 @@ def tile_qwen3attention_pa_kernel(tc, x, wq, wk, wv, q_norm_w, k_norm_w, out_0, 
 
         previous = None
         for kind, i in head_order:
-            if (kind, i) == ("x", 2):
+            if (kind, i) == ("x", 1):
                 make_tables()
             if kind == "x":
                 transpose_x(i)
@@ -231,7 +225,7 @@ def tile_qwen3attention_pa_kernel(tc, x, wq, wk, wv, q_norm_w, k_norm_w, out_0, 
             if previous is not None:
                 (quantize_w if previous[0] == "w" else quantize_x)(previous[1])
             previous = (kind, i)
-        quantize_w(PASSES - 1)
+        quantize_x(TILES - 1)
         for g in range(PASSES):
             for m in range(TILES):
                 matmul(g, m)
@@ -239,39 +233,32 @@ def tile_qwen3attention_pa_kernel(tc, x, wq, wk, wv, q_norm_w, k_norm_w, out_0, 
         interleave_v(PASSES)
         interleave_s(PASSES + 1)
 
-        v_first = BLOCKS - PASSES
-        for s in range(PASSES, v_first):
-            square_sums(s - PASSES)
-            interleave_s(s + 2)
-            inverse_rms(s - PASSES)
-            interleave_v(s + 1)
-            quantize_w(s)
-            for m in range(TILES):
-                matmul(s, m)
-            if s > PASSES + 1:
-                rope_sums(nc.gpsimd, s - PASSES - 2)
-            if s > PASSES:
-                rope_products(s - PASSES - 1)
+        def bank_step(b, m):
+            return (b // PASSES) * TILES + m - BANKS + ROPE_LAG if b >= 2 * PASSES else 0
 
-        for s in range(v_first, BLOCKS):
+        waiting = []
+        for s in range(PASSES, ROPED + ROPE_LAG):
+            if 0 <= s - STATS_LAG < ROPED:
+                square_sums(s - STATS_LAG)
             if s + 2 < BLOCKS:
                 interleave_s(s + 2)
+            if s >= BLOCKS:
+                copy_out_v(ROPED + s - BLOCKS)
+            if 0 <= s - STATS_LAG < ROPED:
+                inverse_rms(s - STATS_LAG)
             if s + 1 < BLOCKS:
                 interleave_v(s + 1)
-            quantize_w(s)
-            for m in range(TILES - 1):
-                matmul(s, m)
-        q_last = ROPED - TILES
-        rope_sums(nc.gpsimd, q_last - 2)
-        rope_products(q_last - 1)
-        for s in range(v_first, BLOCKS):
-            matmul(s, TILES - 1)
-        for m in range(TILES):
-            square_sums(q_last + m)
-            if m > 0:
-                copy_out_v(ROPED + m - 1)
-            inverse_rms(q_last + m)
-            rope_sums(nc.gpsimd, q_last + m - 1)
-            rope_products(q_last + m)
-        copy_out_v(ROPED + TILES - 1)
+            if s < BLOCKS:
+                quantize_w(s)
+                waiting.extend((s, m) for m in range(TILES))
+            for b, m in [bm for bm in waiting if bank_step(*bm) < s]:
+                matmul(b, m)
+                waiting.remove((b, m))
+            if s > ROPE_LAG:
+                rope_sums(nc.gpsimd, s - ROPE_LAG - 1)
+            if s >= ROPE_LAG:
+                rope_products(s - ROPE_LAG)
+            for b, m in [bm for bm in waiting if bank_step(*bm) == s]:
+                matmul(b, m)
+                waiting.remove((b, m))
         rope_sums(nc.vector, ROPED - 1)

@@ -30,8 +30,9 @@ CHUNKS = (H + 2 * KV) * DH // N
 BLOCKS = CHUNKS * PASSES
 ROPED = (CHUNKS - 1) * TILES
 RUN = 4
-V_HEAD = 360
-V_STEADY = 200
+V_HEAD = 320
+V_FILL = 288
+V_STEADY = 184
 STATS_LAG = 6
 ROPE_LAG = 8
 BANKS = 8
@@ -118,7 +119,9 @@ def tile_qwen3attention_pa_kernel(tc, x, wq, wk, wv, q_norm_w, k_norm_w, out_0, 
                         op=ALU.mult)
 
         def v_share(b):
-            return V_HEAD if b <= ROPE_LAG + 1 else V_STEADY
+            if b < PASSES:
+                return V_HEAD
+            return V_FILL if b <= ROPE_LAG + 1 else V_STEADY
 
         def interleave(engine_copy, b, c0, c1):
             if b not in grouped:

import math
from contextlib import ExitStack

import concourse.mybir as mybir
from concourse.masks import make_identity

B, T, D, H, KV, DH = 2, 256, 2048, 16, 4, 128
THETA = 1000000.0
EPS = 1e-6
HALF = DH // 2
FLOPS = 2 * B * T * D * (H + 2 * KV) * DH

F32 = mybir.dt.float32
BF16 = mybir.dt.bfloat16
I32 = mybir.dt.int32
U32 = mybir.dt.uint32
U8 = mybir.dt.uint8
E5M2X4 = mybir.dt.float8_e5m2_x4
ALU = mybir.AluOpType
ACT = mybir.ActivationFunctionType

P = 128
PACK = 4
K_PASS = P * PACK
PASSES = D // K_PASS
N = 512
HEADS = N // DH
TILES = B * T // P
CHUNKS = (H + 2 * KV) * DH // N
BLOCKS = CHUNKS * PASSES
ROPED = (CHUNKS - 1) * TILES
RUN = 4
V_HEAD = 320
V_FILL = 288
V_STEADY = 184
STATS_LAG = 6
ROPE_LAG = 8
BANKS = 8


def tile_qwen3attention_pa_kernel(tc, x, wq, wk, wv, q_norm_w, k_norm_w, out_0, out_1, out_2):
    nc = tc.nc
    x_rows = x.rearrange("b t d -> (b t) d")
    q_rows = out_0.rearrange("b t h d -> (b t) (h d)")
    k_rows = out_1.rearrange("b t h d -> (b t) (h d)")
    v_rows = out_2.rearrange("b t h d -> (b t) (h d)")
    q_chunks = H * DH // N
    chunk_w = [wk] + [wq[:, c * N:(c + 1) * N] for c in range(q_chunks)] + [wv]
    chunk_out = [k_rows] + [q_rows[:, c * N:(c + 1) * N] for c in range(q_chunks)] + [v_rows]

    with ExitStack() as ctx:
        keep = ctx.enter_context(tc.tile_pool(name="keep", bufs=1))
        work = ctx.enter_context(tc.tile_pool(name="work", bufs=2))
        psum = ctx.enter_context(tc.psum_pool(name="psum", bufs=1))
        ctx.enter_context(tc.manual_schedule())

        w_raw, x_raw = {}, {}
        grouped, w_codes, w_scales = {}, {}, {}
        x_grouped, x_codes, x_scales = {}, {}, {}
        acc, sum_sq, rstd, prod, result = {}, {}, {}, {}, {}

        def load_w(b):
            c, g = divmod(b, PASSES)
            w_raw[b] = keep.tile([P, PACK, N], BF16, name="w_raw", tag="slot%d" % b, align_bytes=64)
            rows = chunk_w[c][g * K_PASS:(g + 1) * K_PASS, :]
            nc.sync.dma_start(out=w_raw[b][:], in_=rows.rearrange("(p j) n -> p j n", j=PACK))

        def load_x(m):
            x_raw[m] = keep.tile([P, D], BF16, name="x_raw%d" % m, align_bytes=64)
            nc.sync.dma_start(out=x_raw[m][:], in_=x_rows[m * P:(m + 1) * P, :])

        head_order = [(kind, i) for i in range(TILES) for kind in ("w", "x")]
        for kind, i in head_order:
            (load_w if kind == "w" else load_x)(i)
        for b in range(PASSES, BLOCKS):
            load_w(b)

        pos = keep.tile([P, 2], I32, name="pos")
        nc.gpsimd.iota(pos[:], pattern=[[P, 2]], base=0, channel_multiplier=1)
        norm_rows = keep.tile([P, 2, DH], BF16, name="norm_rows")
        nc.vector.memset(norm_rows[:], 0.0)
        ones = keep.tile([P, P], BF16, name="ones")
        nc.vector.memset(ones[:], 1.0)
        nc.scalar.dma_start(out=norm_rows[0:1, 0, :], in_=k_norm_w.rearrange("(o d) -> o d", o=1))
        nc.scalar.dma_start(out=norm_rows[0:1, 1, :], in_=q_norm_w.rearrange("(o d) -> o d", o=1))
        ident = keep.tile([P, P], F32, name="ident")
        make_identity(nc, ident[:])

        ratio = THETA ** (-2.0 / DH)
        low = keep.tile([P, 2, 8], F32, name="low")
        for j in range(8):
            nc.vector.tensor_scalar(out=low[:, :, j], in0=pos[:], scalar1=ratio ** j / (2 * math.pi), scalar2=None,
                                    op0=ALU.mult)
        turns = keep.tile([P, 2, HALF], F32, name="turns")
        for a in range(8):
            nc.vector.tensor_scalar(out=turns[:, :, 8 * a:8 * a + 8], in0=low[:], scalar1=ratio ** (8 * a),
                                    scalar2=None, op0=ALU.mult)
        whole = keep.tile([P, 2, 2, HALF], I32, name="whole")
        frac = keep.tile([P, 2, 3, HALF], F32, name="frac")
        for cs, shift in enumerate((0.25, 0.0)):
            nc.vector.tensor_scalar(out=whole[:, :, cs, :], in0=turns[:], scalar1=shift, scalar2=None, op0=ALU.add)
        for cs, shift in enumerate((0.25, 0.0)):
            nc.vector.scalar_tensor_tensor(out=frac[:, :, cs, :], in0=turns[:], scalar=shift, in1=whole[:, :, cs, :],
                                           op0=ALU.add, op1=ALU.subtract)
        nc.vector.tensor_tensor(out=frac[:, :, 2, :], in0=whole[:, :, 1, :], in1=turns[:], op=ALU.subtract)
        trig = keep.tile([P, 2, 3, HALF], F32, name="trig")
        nc.scalar.activation(out=trig[:], in_=frac[:], func=ACT.Sin, scale=2 * math.pi)
        table = keep.tile([P, 2, 2, 2, 2, HALF], F32, name="table")

        def make_tables():
            norm_w = psum.tile([P, 2, 2, HALF], F32, name="norm_w", tag="bank0")
            nc.tensor.matmul(out=norm_w[:].rearrange("p w s j -> p (w s j)"), lhsT=ones[:],
                             rhs=norm_rows[:].rearrange("p w d -> p (w d)"), start=True, stop=True)
            for w in range(2):
                for side in range(2):
                    nc.vector.tensor_tensor(
                        out=table[:, w, :, side], in0=trig[:, :, 0:side + 2:side + 1, :],
                        in1=norm_w[:, w, side, :].unsqueeze(1).unsqueeze(1).to_broadcast([P, 2, 2, HALF]),
                        op=ALU.mult)

        def v_share(b):
            if b < PASSES:
                return V_HEAD
            return V_FILL if b <= ROPE_LAG + 1 else V_STEADY

        def interleave(engine_copy, b, c0, c1):
            if b not in grouped:
                grouped[b] = work.tile([P, N, PACK], BF16, name="grouped", bufs=4, align_bytes=64)
            engine_copy(out=grouped[b][:, c0:c1, :].rearrange("p (c i) t -> p c t i", i=RUN),
                        in_=w_raw[b][:, :, c0:c1].rearrange("p t (c i) -> p c t i", i=RUN))

        def interleave_v(b):
            interleave(nc.vector.tensor_copy, b, 0, v_share(b))

        def interleave_s(b):
            interleave(nc.scalar.copy, b, v_share(b), N)

        def quantize_w(b):
            w_codes[b] = work.tile([P, N], U32, name="w_codes", bufs=6, align_bytes=64)
            w_scales[b] = work.tile([P, N], U8, name="w_scales", bufs=6, align_bytes=64)
            nc.vector.quantize_mx(out=w_codes[b][:].bitcast(E5M2X4), scales=w_scales[b][:],
                                  in_=grouped[b][:].rearrange("p n t -> p (n t)"))

        def transpose_x(m):
            words = x_raw[m][:].bitcast(F32)
            x_grouped[m] = work.tile([P, PASSES, P, PACK], BF16, name="x_grouped", bufs=2, align_bytes=64)
            for gp in range(PASSES // 2):
                bank = psum.tile([P, 2, 2, P], F32, name="xt", tag="bank%d" % (TILES + 2 * (m % 2) + gp))
                for gl in range(2):
                    g = 2 * gp + gl
                    for u in range(2):
                        nc.tensor.transpose(bank[:, gl, u, :], words[:, 256 * g + u:256 * (g + 1):2], ident[:])
                dst = x_grouped[m][:, 2 * gp:2 * gp + 2].rearrange("p g r t -> p (g r t)").bitcast(F32)
                nc.scalar.copy(out=dst.rearrange("p (g r u) -> p g r u", g=2, u=2),
                               in_=bank[:].rearrange("p g u r -> p g r u"))

        def quantize_x(m):
            x_codes[m] = keep.tile([P, PASSES, P], U32, name="x_codes%d" % m, align_bytes=64)
            x_scales[m] = keep.tile([P, PASSES, P], U8, name="x_scales%d" % m, align_bytes=64)
            nc.vector.quantize_mx(out=x_codes[m][:].rearrange("p g r -> p (g r)").bitcast(E5M2X4),
                                  scales=x_scales[m][:].rearrange("p g r -> p (g r)"),
                                  in_=x_grouped[m][:].rearrange("p g r t -> p (g r t)"))

        def matmul(b, m):
            c, g = divmod(b, PASSES)
            i = c * TILES + m
            if g == 0:
                acc[i] = psum.tile([P, N], F32, name="acc", tag="bank%d" % (i % (2 * TILES)))
            nc.tensor.matmul_mx(out=acc[i][:], lhsT=x_codes[m][:, g, :].bitcast(E5M2X4), lhsT_scale=x_scales[m][:, g, :],
                                rhs=w_codes[b][:].bitcast(E5M2X4), rhs_scale=w_scales[b][:],
                                start=(g == 0), stop=(g == PASSES - 1))

        def square_sums(i):
            sum_sq[i] = work.tile([P, HEADS], F32, name="sum_sq", bufs=3)
            squares = work.tile([P, HEADS, DH], F32, name="squares", bufs=2)
            for h in range(HEADS):
                nc.scalar.activation(out=squares[:, h, :], in_=acc[i][:, h * DH:(h + 1) * DH], func=ACT.Square,
                                     accum_out=sum_sq[i][:, h:h + 1])

        def inverse_rms(i):
            rstd[i] = work.tile([P, HEADS], F32, name="rstd", bufs=4)
            nc.scalar.activation(out=rstd[i][:], in_=sum_sq[i][:], func=ACT.Abs_reciprocal_sqrt,
                                 scale=1.0 / DH, bias=EPS)

        def rope_products(i):
            c, m = divmod(i, TILES)
            w = min(c, 1)
            half = m % 2
            prod[i] = work.tile([P, 2, N], F32, name="prod", bufs=3)
            halves = prod[i][:].rearrange("p a (s j) -> p (a s) j", j=HALF)
            for h in range(HEADS):
                for side in range(2):
                    own = 2 * h + side
                    partner = 2 * HEADS + 2 * h + 1 - side
                    nc.vector.scalar_tensor_tensor(
                        out=halves[:, own:partner + 1:partner - own, :],
                        in0=acc[i][:, own * HALF:(own + 1) * HALF].unsqueeze(1).to_broadcast([P, 2, HALF]),
                        scalar=rstd[i][:, h:h + 1], in1=table[:, w, half, side],
                        op0=ALU.mult, op1=ALU.mult)

        def result_tile(i):
            tag = "slot%d" % ((i + ROPE_LAG + 2) % BLOCKS)
            result[i] = keep.tile([P, N], F32, name="result", tag=tag, align_bytes=64)

        def store(i):
            c, m = divmod(i, TILES)
            nc.sync.dma_start(out=chunk_out[c][m * P:(m + 1) * P, :], in_=result[i][:])

        def rope_sums(engine, i):
            result_tile(i)
            engine.tensor_tensor(out=result[i][:], in0=prod[i][:, 0, :], in1=prod[i][:, 1, :], op=ALU.add)
            store(i)

        def copy_out_v(i):
            result_tile(i)
            nc.scalar.copy(out=result[i][:], in_=acc[i][:])
            store(i)

        previous = None
        for kind, i in head_order:
            if (kind, i) == ("x", 1):
                make_tables()
            if kind == "x":
                transpose_x(i)
            else:
                interleave_s(i)
                interleave_v(i)
            if previous is not None:
                (quantize_w if previous[0] == "w" else quantize_x)(previous[1])
            previous = (kind, i)
        quantize_x(TILES - 1)
        for g in range(PASSES):
            for m in range(TILES):
                matmul(g, m)
        interleave_s(PASSES)
        interleave_v(PASSES)
        interleave_s(PASSES + 1)

        def bank_step(b, m):
            return (b // PASSES) * TILES + m - BANKS + ROPE_LAG if b >= 2 * PASSES else 0

        waiting = []
        for s in range(PASSES, ROPED + ROPE_LAG):
            if 0 <= s - STATS_LAG < ROPED:
                square_sums(s - STATS_LAG)
            if s + 2 < BLOCKS:
                interleave_s(s + 2)
            if s >= BLOCKS:
                copy_out_v(ROPED + s - BLOCKS)
            if 0 <= s - STATS_LAG < ROPED:
                inverse_rms(s - STATS_LAG)
            if s + 1 < BLOCKS:
                interleave_v(s + 1)
            if s < BLOCKS:
                quantize_w(s)
                waiting.extend((s, m) for m in range(TILES))
            for b, m in [bm for bm in waiting if bank_step(*bm) < s]:
                matmul(b, m)
                waiting.remove((b, m))
            if s > ROPE_LAG:
                rope_sums(nc.gpsimd, s - ROPE_LAG - 1)
            if s >= ROPE_LAG:
                rope_products(s - ROPE_LAG)
            for b, m in [bm for bm in waiting if bank_step(*bm) == s]:
                matmul(b, m)
                waiting.remove((b, m))
        rope_sums(nc.vector, ROPED - 1)
